import numpy as np
import ml_dtypes


def mxq(x, axis, fmt="e4m3"):
    dtype, down = {"e4m3": (ml_dtypes.float8_e4m3fn, 7), "e5m2": (ml_dtypes.float8_e5m2, 14)}[fmt]
    v = np.moveaxis(np.asarray(x, np.float32).astype(ml_dtypes.bfloat16).astype(np.float64), axis, -1)
    blocks = v.reshape(v.shape[:-1] + (-1, 32))
    amax = np.abs(blocks).max(-1, keepdims=True)
    byte = np.maximum(np.where(amax > 0, np.frexp(amax)[1] - 1 + 127, 0) - down, 1)
    scale = np.exp2(byte - 127.0)
    codes = (blocks / scale).astype(np.float32).astype(dtype).astype(np.float64)
    return np.moveaxis((codes * scale).reshape(v.shape), -1, axis)


WIDE = False


def mx_kscale(k):
    if not WIDE:
        return np.ones(k)
    levels = np.array([10, -10, 5, -5, 0])
    if k % 512:
        return np.exp2(np.random.permutation(np.resize(levels, k // 32))).repeat(32)
    a = np.empty((k // 512, 16))
    for p in range(k // 512):
        a[p, :8] = np.random.permutation(np.resize(levels, 8))
        for g in range(8):
            far = levels[np.abs(levels - a[p, g]) >= 10]
            a[p, g + 8] = far[np.random.randint(len(far))]
    return np.exp2(a.ravel()).repeat(32)


BF16 = ml_dtypes.bfloat16


def bf(x):
    return np.asarray(x, np.float32).astype(BF16)


def f64(x):
    return np.asarray(x).astype(np.float64)


N, D, H, E = 1024, 512, 2048, 8

CLAMP_MAX = float(np.log(100.0))


def setup_inputs():
    s, t = mx_kscale(D), mx_kscale(H)
    return {"x": bf(np.random.standard_normal((N, D)) * s),
            "W1": bf(np.random.standard_normal((E, D, H)) / np.sqrt(D) / s[:, None] * t),
            "b1": bf(np.random.standard_normal((E, H)) * 0.1 * t),
            "W2": bf(np.random.standard_normal((E, H, D)) / np.sqrt(H) / t[:, None]),
            "b2": bf(np.random.standard_normal((E, D)) * 0.1),
            "temperature": bf(np.log(2.0) + 0.1 * np.random.standard_normal((1,)))}


def reference(x, W1, b1, W2, b2, temperature):
    xe = f64(x).reshape(E, N // E, D)
    h = np.maximum((mxq(xe, 2, "e4m3") @ mxq(f64(W1), 1, "e4m3")) + f64(b1)[:, None, :], 0.0)
    y = (mxq(h, 2, "e4m3") @ mxq(f64(W2), 1, "e4m3")) + f64(b2)[:, None, :]
    logit_scale = np.exp(np.minimum(f64(temperature), CLAMP_MAX))
    return y.reshape(N, D) * logit_scale

from contextlib import ExitStack
import math

import concourse.mybir as mybir
from concourse.masks import make_identity

N_TOK, D, H, E = 1024, 512, 2048, 8
FLOPS = 4 * N_TOK * D * H

F32 = mybir.dt.float32
BF16 = mybir.dt.bfloat16
U32 = mybir.dt.uint32
U8 = mybir.dt.uint8
FP8X4 = mybir.dt.float8_e4m3fn_x4
ALU = mybir.AluOpType
ACT = mybir.ActivationFunctionType

P = 128
PACK = 4
N_TILE = 512
UNITS = 4
CLAMP_MAX = math.log(100.0)

RAW_BUFS = 7
SCALAR_UNITS = 35
SCALAR_LEAD = 3
VECTOR_LEAD = 1
X_TURN = 6
X_COPY = 4
X_QUANT = 1
BANK_LAG = 2
BIAS_LAG = 4
M2_LAG = 2
FAST = True
EARLY = 3


def tile_moelayer_kernel(tc, x, W1, b1, W2, b2, temperature, out):
    nc = tc.nc

    stream = [(1, 0, q) for q in range(UNITS)]
    for e in range(1, E):
        stream.extend([(1, e, q) for q in range(UNITS)])
        stream.extend([(2, e - 1, q) for q in range(UNITS)])
    stream.extend([(2, E - 1, q) for q in range(UNITS)])
    n_units = len(stream)

    def unit(n):
        return stream[n] if 0 <= n < n_units else (0, 0, 0)

    def on_scalar(n):
        return ((n + 1) * SCALAR_UNITS) // n_units > (n * SCALAR_UNITS) // n_units

    with ExitStack() as ctx:
        const = ctx.enter_context(tc.tile_pool(name="const", bufs=1))
        work = ctx.enter_context(tc.tile_pool(name="work", bufs=2))
        psum = ctx.enter_context(tc.psum_pool(name="psum", bufs=8))
        ctx.enter_context(tc.manual_schedule())

        raw_unit = {}
        grouped = {}
        codes = {}
        scales = {}
        bank = {}
        turned = {}
        h_rows = {}
        x_rows = {}
        x_turned = {}
        x_grouped = {}
        x_codes = {}
        x_scales = {}
        h_biased = {}
        h_relu = {}
        h_codes = {}
        h_scales = {}
        acc = {}
        b2_rows = {}
        b2_scaled = {}

        def load_matrix(w):
            kind, e, q0 = stream[UNITS * w]
            if kind == 1:
                x_rows[e] = work.tile([P, D], BF16, tag="x_rows", name="x_rows", bufs=E)
                queue = nc.scalar if w == 0 else nc.sync
                queue.dma_start(out=x_rows[e][:], in_=x[e * P : (e + 1) * P, :])
                raw = work.tile([P, PACK, H], BF16, tag="raw", name="raw", bufs=RAW_BUFS)
                src = W1[e].rearrange("(p j) h -> p j h", j=PACK)
                pieces = UNITS if w < EARLY else 1
                width = H // pieces
                for c in range(pieces):
                    cols = slice(c * width, (c + 1) * width)
                    nc.sync.dma_start(out=raw[:, :, cols], in_=src[:, :, cols])
                for q in range(UNITS):
                    raw_unit[UNITS * w + q] = raw[:, :, q * N_TILE : (q + 1) * N_TILE]
            else:
                b2_rows[e] = work.tile([P, D], BF16, tag="b2_rows", name="b2_rows", bufs=E)
                nc.sync.dma_start(out=b2_rows[e][:], in_=b2[e].partition_broadcast(P))
                raw = work.tile([P, UNITS, PACK, D], BF16, tag="raw", name="raw", bufs=RAW_BUFS)
                src = W2[e].rearrange("(g p j) d -> p g j d", g=UNITS, j=PACK)
                pieces = UNITS if w < EARLY else 1
                width = UNITS // pieces
                for c in range(pieces):
                    rows = slice(c * width, (c + 1) * width)
                    nc.sync.dma_start(out=raw[:, rows], in_=src[:, rows])
                for q in range(UNITS):
                    raw_unit[UNITS * w + q] = raw[:, q]

        def interleave(n):
            g = work.tile([P, N_TILE, PACK], BF16, tag="grouped", name="grouped", bufs=6, align_bytes=64)
            grouped[n] = g
            if FAST:
                dst = g.rearrange("p (c i) j -> p c j i", i=4)
                src = raw_unit[n].rearrange("p j (c i) -> p c j i", i=4)
            else:
                dst = g[:]
                src = raw_unit[n].rearrange("p j c -> p c j")
            if on_scalar(n):
                nc.scalar.copy(out=dst, in_=src)
            else:
                nc.vector.tensor_copy(out=dst, in_=src)

        def quantize(n):
            codes[n] = work.tile([P, N_TILE], U32, tag="codes", name="codes", bufs=6, align_bytes=64)
            scales[n] = work.tile([P, N_TILE], U8, tag="scales", name="scales", bufs=6, align_bytes=64)
            nc.vector.quantize_mx(
                out=codes[n][:].bitcast(FP8X4),
                scales=scales[n][:],
                in_=grouped[n].rearrange("p c j -> p (c j)"),
            )

        def multiply(n):
            kind, e, q = stream[n]
            if kind == 1:
                bank[n] = psum.tile([P, N_TILE], F32, tag="bank", name="bank")
                nc.tensor.matmul_mx(
                    out=bank[n][:],
                    lhsT=x_codes[e][:].bitcast(FP8X4),
                    lhsT_scale=x_scales[e][:],
                    rhs=codes[n][:].bitcast(FP8X4),
                    rhs_scale=scales[n][:],
                    start=True,
                    stop=True,
                )
            else:
                if q == 0:
                    acc[e] = psum.tile([P, D], F32, tag="bank", name="acc")
                nc.tensor.matmul_mx(
                    out=acc[e][:],
                    lhsT=h_codes[e][:, q, :].bitcast(FP8X4),
                    lhsT_scale=h_scales[e][:, q, :],
                    rhs=codes[n][:].bitcast(FP8X4),
                    rhs_scale=scales[n][:],
                    start=(q == 0),
                    stop=(q == UNITS - 1),
                )

        def empty_bank(n):
            h_rows[n] = work.tile([P, PACK, P], F32, tag="h_rows", name="h_rows", bufs=3)
            nc.scalar.copy(out=h_rows[n][:], in_=bank[n].rearrange("r (m t) -> r t m", t=PACK))

        def turn(n):
            turned[n] = psum.tile([P, PACK, P], F32, tag="bank", name="turned")
            for t in range(PACK):
                nc.tensor.transpose(out=turned[n][:, t, :], in_=h_rows[n][:, t, :], identity=ident[:])

        def add_bias(n):
            kind, e, q = stream[n]
            if q == 0:
                h_biased[e] = work.tile([P, UNITS, P, PACK], BF16, tag="h_biased", name="h_biased", bufs=2)
            row = UNITS * e + q
            nc.vector.tensor_tensor(
                out=h_biased[e][:, q],
                in0=turned[n].rearrange("p t r -> p r t"),
                in1=b1_grouped[:, row : row + 1, :].to_broadcast([P, P, PACK]),
                op=ALU.add,
            )

        def relu(e):
            h_relu[e] = work.tile([P, UNITS, P, PACK], BF16, tag="h_relu", name="h_relu", bufs=2, align_bytes=64)
            nc.vector.tensor_scalar_max(
                out=h_relu[e].rearrange("p q r t -> p (q r t)"),
                in0=h_biased[e].rearrange("p q r t -> p (q r t)"),
                scalar1=0.0,
            )

        def quantize_h(e):
            h_codes[e] = work.tile([P, UNITS, P], U32, tag="h_codes", name="h_codes", bufs=2, align_bytes=64)
            h_scales[e] = work.tile([P, UNITS, P], U8, tag="h_scales", name="h_scales", bufs=2, align_bytes=64)
            nc.vector.quantize_mx(
                out=h_codes[e].rearrange("p q r -> p (q r)").bitcast(FP8X4),
                scales=h_scales[e].rearrange("p q r -> p (q r)"),
                in_=h_relu[e].rearrange("p q r t -> p (q r t)"),
            )

        def scale_b2(e):
            b2_scaled[e] = work.tile([P, D], F32, tag="b2_scaled", name="b2_scaled", bufs=2)
            nc.scalar.activation(out=b2_scaled[e][:], in_=b2_rows[e][:], func=ACT.Copy, scale=logit_scale[:, 0:1])

        def finish(e):
            res = work.tile([P, D], F32, tag="res", name="res", bufs=2)
            nc.vector.scalar_tensor_tensor(
                out=res[:],
                in0=acc[e][:],
                scalar=logit_scale[:, 0:1],
                in1=b2_scaled[e][:],
                op0=ALU.mult,
                op1=ALU.add,
            )
            nc.sync.dma_start(out=out[e * P : (e + 1) * P, :], in_=res[:])

        def turn_words(rows):
            words = rows[:].bitcast(F32)
            t = psum.tile([P, 2, P], F32, tag="bank", name="words")
            for u in range(2):
                nc.tensor.transpose(out=t[:, u, :], in_=words[:, u::2], identity=ident[:])
            return t

        def quantize_x(e):
            x_codes[e] = work.tile([P, P], U32, tag="x_codes", name="x_codes", bufs=2, align_bytes=64)
            x_scales[e] = work.tile([P, P], U8, tag="x_scales", name="x_scales", bufs=2, align_bytes=64)
            nc.vector.quantize_mx(
                out=x_codes[e][:].bitcast(FP8X4),
                scales=x_scales[e][:],
                in_=x_grouped[e].rearrange("p r t -> p (r t)"),
            )

        zero = const.tile([P, 1], F32, tag="zero", name="zero")
        warm = const.tile([P, 1], F32, tag="warm", name="warm")
        temp = const.tile([P, 1], BF16, tag="temp", name="temp")
        clamped = const.tile([P, 1], F32, tag="clamped", name="clamped")
        logit_scale = const.tile([P, 1], F32, tag="logit_scale", name="logit_scale")
        ident = const.tile([P, P], F32, tag="ident", name="ident")
        b1_rows = const.tile([P, D], BF16, tag="b1_rows", name="b1_rows")
        b1_grouped = const.tile([P, P, PACK], BF16, tag="b1_grouped", name="b1_grouped")

        nc.gpsimd.memset(zero[:], 0.0)
        nc.gpsimd.memset(b1_rows[:], 0.0)
        make_identity(nc, ident[:])
        for w in range(RAW_BUFS):
            load_matrix(w)
        nc.scalar.dma_start(out=temp[:], in_=temperature.partition_broadcast(P))
        nc.scalar.activation(out=warm[:], in_=zero[:], func=ACT.Exp)
        nc.scalar.dma_start(out=b1_rows[0 : E * UNITS, :], in_=b1.rearrange("e (q c) -> (e q) c", q=UNITS))

        b1_turned = {}
        for s in range(-X_TURN, n_units + M2_LAG + 2):
            if unit(s - BANK_LAG)[0] == 1:
                empty_bank(s - BANK_LAG)
            kind, e, q = unit(s + X_COPY)
            if kind == 1 and q == 0:
                x_grouped[e] = work.tile([P, P, PACK], BF16, tag="x_grouped", name="x_grouped", bufs=2, align_bytes=64)
                nc.scalar.copy(out=x_grouped[e][:].bitcast(F32), in_=x_turned[e].rearrange("p u r -> p r u"))
            if s == 2:
                nc.scalar.activation(out=logit_scale[:], in_=clamped[:], func=ACT.Exp)
            kind, e, q = unit(s)
            if kind == 2 and q == 0:
                scale_b2(e)
            if unit(s + SCALAR_LEAD)[0] and on_scalar(s + SCALAR_LEAD):
                interleave(s + SCALAR_LEAD)
            if unit(s + VECTOR_LEAD)[0] and not on_scalar(s + VECTOR_LEAD):
                interleave(s + VECTOR_LEAD)
            if unit(s)[0]:
                quantize(s)
            if s == 1:
                nc.vector.tensor_scalar_min(out=clamped[:], in0=temp[:], scalar1=CLAMP_MAX)
            if s == 3:
                nc.vector.tensor_copy(out=b1_grouped[:].bitcast(F32), in_=b1_turned[0].rearrange("p u r -> p r u"))
            if unit(s - BIAS_LAG)[0] == 1:
                add_bias(s - BIAS_LAG)
            kind, e, q = unit(s - BIAS_LAG - 1)
            if kind == 1 and q == UNITS - 1:
                relu(e)
            kind, e, q = unit(s - BIAS_LAG - 2)
            if kind == 1 and q == UNITS - 1:
                quantize_h(e)
            kind, e, q = unit(s + X_QUANT)
            if kind == 1 and q == 0:
                quantize_x(e)
            kind, e, q = unit(s - M2_LAG - 1)
            if kind == 2 and q == UNITS - 1:
                finish(e)
            kind, e, q = unit(s + X_TURN)
            if kind == 1 and q == 0:
                x_turned[e] = turn_words(x_rows[e])
            if s == 1:
                b1_turned[0] = turn_words(b1_rows)
            if unit(s - BANK_LAG)[0] == 1:
                turn(s - BANK_LAG)
            if unit(s)[0] == 1:
                multiply(s)
            if unit(s - M2_LAG)[0] == 2:
                multiply(s - M2_LAG)
            if s >= 0 and s % UNITS == UNITS - 1 and s // UNITS + RAW_BUFS < 2 * E:
                load_matrix(s // UNITS + RAW_BUFS)
